import numpy as np
import ml_dtypes


def mxq(x, axis, fmt="e4m3"):
    dtype, down = {"e4m3": (ml_dtypes.float8_e4m3fn, 7), "e5m2": (ml_dtypes.float8_e5m2, 14)}[fmt]
    v = np.moveaxis(np.asarray(x, np.float32).astype(ml_dtypes.bfloat16).astype(np.float64), axis, -1)
    blocks = v.reshape(v.shape[:-1] + (-1, 32))
    amax = np.abs(blocks).max(-1, keepdims=True)
    byte = np.maximum(np.where(amax > 0, np.frexp(amax)[1] - 1 + 127, 0) - down, 1)
    scale = np.exp2(byte - 127.0)
    codes = (blocks / scale).astype(np.float32).astype(dtype).astype(np.float64)
    return np.moveaxis((codes * scale).reshape(v.shape), -1, axis)


WIDE = False


def mx_kscale(k):
    if not WIDE:
        return np.ones(k)
    levels = np.array([10, -10, 5, -5, 0])
    a = np.random.permutation(np.resize(levels, k // 512 * 4)).reshape(k // 512, 4)
    idx = np.arange(k)
    return np.exp2(a[idx // 512, idx % 128 // 32])


BF16 = ml_dtypes.bfloat16


def bf(x):
    return np.asarray(x, np.float32).astype(BF16)


def f64(x):
    return np.asarray(x).astype(np.float64)


B, T, C, NH, HS, NLQ, NLKV, DHR = 1, 512, 2048, 16, 128, 512, 512, 128
THETA = 10000.0


def rope(v, cos, sin):
    vr = v.reshape(v.shape[:-1] + (-1, 2))
    re, im = vr[..., 0], vr[..., 1]
    c = cos[None, :, None, :]
    s = sin[None, :, None, :]
    return np.stack([re * c - im * s, re * s + im * c], axis=-1).reshape(v.shape)


def setup_inputs():
    s, t = mx_kscale(C), mx_kscale(NLQ)
    ang = np.outer(np.arange(T), 1.0 / THETA ** (np.arange(0, DHR, 2) / DHR))
    return {"x": bf(np.random.standard_normal((B, T, C)) * s),
            "cos": bf(np.cos(ang)),
            "sin": bf(np.sin(ang)),
            "W_dq": bf(np.random.standard_normal((NLQ, C)) / np.sqrt(C) / s[None, :] * t[:, None]),
            "W_uq": bf((np.random.standard_normal((NLQ, C)) / np.sqrt(NLQ) / t[:, None]).reshape(C, NLQ)),
            "W_uk": bf(np.random.standard_normal((C, NLKV)) / np.sqrt(HS)),
            "W_qr": bf(np.random.standard_normal((NH * DHR, NLQ)) / np.sqrt(NLQ) / t[None, :])}


def reference(x, cos, sin, W_dq, W_uq, W_uk, W_qr):
    cq = mxq(mxq(f64(x), 2, "e4m3") @ mxq(f64(W_dq), 1, "e4m3").T, 2, "e4m3")
    k_eff = f64(W_uq).reshape(NLQ, NH, HS).transpose(1, 0, 2) @ f64(W_uk).reshape(NH, HS, NLKV)
    q_abs = cq[:, None] @ mxq(k_eff, 1, "e4m3")[None]
    c_qr = (cq @ mxq(f64(W_qr), 1, "e4m3").T).reshape(B, T, NH, DHR)
    return q_abs, rope(c_qr, f64(cos), f64(sin))

@@ -1,0 +1,239 @@
+from contextlib import ExitStack
+
+import concourse.mybir as mybir
+from concourse.masks import make_identity
+
+F32 = mybir.dt.float32
+BF16 = mybir.dt.bfloat16
+U32 = mybir.dt.uint32
+U8 = mybir.dt.uint8
+FP8X4 = mybir.dt.float8_e4m3fn_x4
+MULT = mybir.AluOpType.mult
+ADD = mybir.AluOpType.add
+
+P = 128
+PACK = 4
+T = 512
+C = 2048
+L = 512
+NH = 16
+HS = 128
+N = 512
+O = 2048
+C_PASSES = C // (P * PACK)
+T_TILES = T // P
+O_BLOCKS = O // 512
+LOOKAHEAD = 2
+VECTOR_EVERY = 3
+
+FLOPS = 2 * (T * C * L + NH * L * HS * N + NH * T * L * N + T * L * O)
+
+
+def tile_causalselfattention_pa_kernel(tc, x, cos, sin, W_dq, W_uq, W_uk, W_qr, out_0, out_1):
+    nc = tc.nc
+    with ExitStack() as ctx:
+        const = ctx.enter_context(tc.tile_pool(name="const", bufs=1))
+        raw = ctx.enter_context(tc.tile_pool(name="raw", bufs=1))
+        codes = ctx.enter_context(tc.tile_pool(name="codes", bufs=1))
+        stage = ctx.enter_context(tc.tile_pool(name="stage", bufs=2))
+        heads = ctx.enter_context(tc.tile_pool(name="heads", bufs=LOOKAHEAD + 2))
+        results = ctx.enter_context(tc.tile_pool(name="results", bufs=2))
+        psum = ctx.enter_context(tc.psum_pool(name="psum", bufs=4))
+
+        wdq_raw = raw.tile([P, PACK, C], BF16)
+        wdq_rows = W_dq.rearrange("(u p e) c -> u p (e c)", u=2, e=2)
+        for u in range(2):
+            nc.sync.dma_start(out=wdq_raw[:, 2 * u : 2 * u + 2, :].rearrange("p e c -> p (e c)"), in_=wdq_rows[u])
+        x_raw = raw.tile([P, T_TILES, C], BF16)
+        x_rows = x.flatten_outer_dims().rearrange("(p r) c -> r p c", r=T_TILES)
+        for r in range(T_TILES):
+            nc.sync.dma_start(out=x_raw[:, r, :], in_=x_rows[r])
+        wuq_raw = raw.tile([P, PACK, NH * HS], BF16)
+        wuq_rows = W_uq.rearrange("(u p k) b -> u p (k b)", u=2, k=8)
+        for u in range(2):
+            nc.sync.dma_start(out=wuq_raw[:, 2 * u : 2 * u + 2, :].rearrange("p e c -> p (e c)"), in_=wuq_rows[u])
+        wuk_raw = raw.tile([P, NH, N], BF16)
+        wuk_rows = W_uk.rearrange("(h d) n -> d h n", d=HS)
+        wqr_raw = raw.tile([P, O // 256, 2 * L], BF16)
+        wqr_rows = W_qr.rearrange("(a p e) l -> p a (e l)", p=P, e=2)
+        cos_raw = const.tile([P, T_TILES, HS // 2], BF16)
+        sin_raw = const.tile([P, T_TILES, HS // 2], BF16)
+        for b in range(O_BLOCKS):
+            nc.sync.dma_start(out=wuk_raw[:, 4 * b : 4 * b + 4, :], in_=wuk_rows[:, 4 * b : 4 * b + 4, :])
+            nc.sync.dma_start(out=wqr_raw[:, 2 * b : 2 * b + 2, :], in_=wqr_rows[:, 2 * b : 2 * b + 2, :])
+            if b == 0:
+                nc.sync.dma_start(out=cos_raw[:], in_=cos.rearrange("(p r) i -> p r i", r=T_TILES))
+                nc.sync.dma_start(out=sin_raw[:], in_=sin.rearrange("(p r) i -> p r i", r=T_TILES))
+
+        ident_f32 = const.tile([P, P], F32)
+        make_identity(nc, ident_f32[:])
+        ident_bf16 = const.tile([P, P], BF16)
+        make_identity(nc, ident_bf16[:])
+
+        cos_pairs = const.tile([P, T_TILES, P, 2], F32)
+        sin_signed = const.tile([P, T_TILES, 2, P], F32)
+        for r in range(T_TILES):
+            nc.gpsimd.tensor_scalar(
+                out=cos_pairs[:, r].rearrange("p (a i) e -> p a i e", a=2),
+                in0=cos_raw[:, r, :].unsqueeze(1).unsqueeze(3).to_broadcast([P, 2, HS // 2, 2]),
+                scalar1=1.0, scalar2=0.0, op0=MULT, op1=ADD,
+            )
+            for e in range(2):
+                nc.gpsimd.tensor_scalar(
+                    out=sin_signed[:, r, e, :].rearrange("p (a i) -> p a i", a=2),
+                    in0=sin_raw[:, r, :].unsqueeze(1).to_broadcast([P, 2, HS // 2]),
+                    scalar1=(-1.0 if e == 0 else 1.0), scalar2=0.0, op0=MULT, op1=ADD,
+                )
+
+        copies = [0]
+
+        def leave_psum(out, in_):
+            if copies[0] % VECTOR_EVERY == VECTOR_EVERY - 1:
+                nc.vector.tensor_copy(out=out, in_=in_)
+            else:
+                nc.scalar.copy(out=out, in_=in_)
+            copies[0] += 1
+
+        def transpose_words(grouped, rows_a, rows_b, tag):
+            bank = psum.tile([P, 2, 2, P], F32, tag=tag, name="words")
+            for run, rows in enumerate((rows_a, rows_b)):
+                for half in range(2):
+                    nc.tensor.transpose(bank[:, run, half, :], rows.bitcast(F32)[:, P * half : P * half + P], ident_f32[:])
+            leave_psum(
+                out=grouped.bitcast(F32).rearrange("p (a c) w -> p a c w", a=2),
+                in_=bank[:].rearrange("p a w c -> p a c w"),
+            )
+
+        def quantise(grouped, words, scales):
+            nc.vector.quantize_mx(out=words.bitcast(FP8X4), scales=scales, in_=grouped.rearrange("p c k -> p (c k)"))
+
+        wdq_words = codes.tile([P, 2, C_PASSES * 2 * P], U32, align_bytes=64)
+        wdq_scales = codes.tile([P, 2, C_PASSES * 2 * P], U8, align_bytes=64)
+        for u in range(2):
+            for pair in range(C_PASSES // 2):
+                wdq_grouped = stage.tile([P, 4 * P, PACK], BF16, align_bytes=64)
+                for g in (2 * pair, 2 * pair + 1):
+                    k_cols = slice(512 * g, 512 * g + 512)
+                    transpose_words(
+                        wdq_grouped[:, 256 * (g % 2) : 256 * (g % 2) + 256, :],
+                        wdq_raw[:, 2 * u, k_cols], wdq_raw[:, 2 * u + 1, k_cols], "a",
+                    )
+                cols = slice(512 * pair, 512 * pair + 512)
+                quantise(wdq_grouped[:], wdq_words[:, u, cols], wdq_scales[:, u, cols])
+
+        x_words = codes.tile([P, T_TILES, C_PASSES * P], U32, align_bytes=64)
+        x_scales = codes.tile([P, T_TILES, C_PASSES * P], U8, align_bytes=64)
+        cq_words = codes.tile([P, T], U32, align_bytes=64)
+        cq_scales = codes.tile([P, T], U8, align_bytes=64)
+        for r in range(T_TILES):
+            x_grouped = stage.tile([P, C_PASSES * P, PACK], BF16, align_bytes=64)
+            for pair in range(C_PASSES // 2):
+                transpose_words(
+                    x_grouped[:, 256 * pair : 256 * pair + 256, :],
+                    x_raw[:, r, 1024 * pair : 1024 * pair + 512], x_raw[:, r, 1024 * pair + 512 : 1024 * pair + 1024], "a",
+                )
+            quantise(x_grouped[:], x_words[:, r, :], x_scales[:, r, :])
+            cq_bank = psum.tile([P, PACK, P], F32, tag="b")
+            for j in range(PACK):
+                for g in range(C_PASSES):
+                    l_cols = slice(256 * g + P * (j % 2), 256 * g + P * (j % 2) + P)
+                    t_cols = slice(P * g, P * g + P)
+                    nc.tensor.matmul_mx(
+                        out=cq_bank[:, j, :],
+                        lhsT=wdq_words[:, j // 2, l_cols].bitcast(FP8X4), lhsT_scale=wdq_scales[:, j // 2, l_cols],
+                        rhs=x_words[:, r, t_cols].bitcast(FP8X4), rhs_scale=x_scales[:, r, t_cols],
+                        start=(g == 0), stop=(g == C_PASSES - 1),
+                    )
+            cq_grouped = stage.tile([P, P, PACK], BF16, align_bytes=64)
+            leave_psum(out=cq_grouped[:], in_=cq_bank[:].rearrange("p j t -> p t j"))
+            quantise(cq_grouped[:], cq_words[:, P * r : P * r + P], cq_scales[:, P * r : P * r + P])
+
+        wqr_words = codes.tile([P, O], U32, align_bytes=64)
+        wqr_scales = codes.tile([P, O], U8, align_bytes=64)
+
+        def quantise_wqr(b):
+            wqr_grouped = stage.tile([P, 512, PACK], BF16, align_bytes=64)
+            for a in range(2):
+                transpose_words(
+                    wqr_grouped[:, 256 * a : 256 * a + 256, :],
+                    wqr_raw[:, 2 * b + a, 0:L], wqr_raw[:, 2 * b + a, L : 2 * L], "b",
+                )
+            cols = slice(512 * b, 512 * b + 512)
+            quantise(wqr_grouped[:], wqr_words[:, cols], wqr_scales[:, cols])
+
+        ke_words = {}
+        ke_scales = {}
+
+        def make_k_eff(h):
+            at_bank = psum.tile([P, PACK, P], BF16, tag="b")
+            for j in range(PACK):
+                nc.tensor.transpose(at_bank[:, j, :], wuq_raw[:, j, HS * h : HS * h + HS], ident_bf16[:])
+            a_t = stage.tile([P, PACK, P], BF16)
+            leave_psum(out=a_t[:], in_=at_bank[:])
+            ke_grouped = stage.tile([P, N, PACK], BF16, align_bytes=64)
+            for n0 in range(0, N, P):
+                ke_bank = psum.tile([P, PACK, P], F32, tag="b")
+                for j in range(PACK):
+                    nc.tensor.matmul(ke_bank[:, j, :], lhsT=a_t[:, j, :], rhs=wuk_raw[:, h, n0 : n0 + P], start=True, stop=True)
+                leave_psum(out=ke_grouped[:, n0 : n0 + P, :], in_=ke_bank[:].rearrange("p j n -> p n j"))
+            ke_words[h] = heads.tile([P, N], U32, align_bytes=64, name="ke_words")
+            ke_scales[h] = heads.tile([P, N], U8, align_bytes=64, name="ke_scales")
+            quantise(ke_grouped[:], ke_words[h][:], ke_scales[h][:])
+
+        q_abs_rows = out_0.flatten_outer_dims().rearrange("(h p r) n -> h p r n", h=NH, r=T_TILES)
+
+        def make_q_abs(h):
+            q_abs = results.tile([P, T_TILES, N], F32, bufs=3)
+            for r in range(T_TILES):
+                qa_bank = psum.tile([P, N], F32, tag="a")
+                nc.tensor.matmul_mx(
+                    out=qa_bank[:],
+                    lhsT=cq_words[:, P * r : P * r + P].bitcast(FP8X4), lhsT_scale=cq_scales[:, P * r : P * r + P],
+                    rhs=ke_words[h][:].bitcast(FP8X4), rhs_scale=ke_scales[h][:],
+                    start=True, stop=True,
+                )
+                leave_psum(out=q_abs[:, r, :], in_=qa_bank[:])
+            nc.sync.dma_start(out=q_abs_rows[h], in_=q_abs[:])
+
+        q_r_rows = out_1.rearrange("b t h d -> (b t) (h d)").rearrange("(p r) o -> p r o", r=T_TILES)
+        q_r = {}
+
+        def make_q_r(b, r):
+            if r == 0:
+                q_r[b] = results.tile([P, T_TILES, 512], F32, name="q_r")
+            cols = slice(512 * b, 512 * b + 512)
+            cr_bank = psum.tile([P, 2, 2, P], F32, tag="a")
+            nc.tensor.matmul_mx(
+                out=cr_bank[:].rearrange("p a e c -> p (a e c)"),
+                lhsT=cq_words[:, P * r : P * r + P].bitcast(FP8X4), lhsT_scale=cq_scales[:, P * r : P * r + P],
+                rhs=wqr_words[:, cols].bitcast(FP8X4), rhs_scale=wqr_scales[:, cols],
+                start=True, stop=True,
+            )
+            same = results.tile([P, 2, P, 2], F32)
+            nc.vector.tensor_tensor(
+                out=same[:], in0=cr_bank[:].rearrange("p a e c -> p a c e"),
+                in1=cos_pairs[:, r].unsqueeze(1).to_broadcast([P, 2, P, 2]), op=MULT,
+            )
+            cross = results.tile([P, 2, 2, P], F32)
+            for e in range(2):
+                nc.vector.tensor_tensor(
+                    out=cross[:, e], in0=cr_bank[:, :, 1 - e, :],
+                    in1=sin_signed[:, r, e, :].unsqueeze(1).to_broadcast([P, 2, P]), op=MULT,
+                )
+            nc.gpsimd.tensor_tensor(
+                out=q_r[b][:, r, :].rearrange("p (a c e) -> p a c e", a=2, e=2),
+                in0=same[:], in1=cross[:].rearrange("p e a c -> p a c e"), op=ADD,
+            )
+            if r == T_TILES - 1:
+                nc.sync.dma_start(out=q_r_rows[:, :, cols], in_=q_r[b][:])
+
+        for h in range(LOOKAHEAD):
+            make_k_eff(h)
+        quantise_wqr(0)
+        for h in range(NH):
+            if h + LOOKAHEAD < NH:
+                make_k_eff(h + LOOKAHEAD)
+            make_q_abs(h)
+            make_q_r(h // T_TILES, h % T_TILES)
+            if h % T_TILES == 1 and h // T_TILES + 1 < O_BLOCKS:
+                quantise_wqr(h // T_TILES + 1)

@@ -22,9 +22,12 @@ N = 512
 O = 2048
 C_PASSES = C // (P * PACK)
 T_TILES = T // P
-O_BLOCKS = O // 512
-LOOKAHEAD = 2
-VECTOR_EVERY = 3
+BANK = 512
+O_BLOCKS = O // BANK
+FIRST_HEADS = 4
+QA_BANKS = ("qa", 3)
+KE_BANKS = ("ke", 3)
+TP_BANKS = ("tp", 1)
 
 FLOPS = 2 * (T * C * L + NH * L * HS * N + NH * T * L * N + T * L * O)
 
@@ -32,38 +35,47 @@ FLOPS = 2 * (T * C * L + NH * L * HS * N + NH * T * L * N + T * L * O)
 def tile_causalselfattention_pa_kernel(tc, x, cos, sin, W_dq, W_uq, W_uk, W_qr, out_0, out_1):
     nc = tc.nc
     with ExitStack() as ctx:
+        ctx.enter_context(tc.manual_schedule())
         const = ctx.enter_context(tc.tile_pool(name="const", bufs=1))
         raw = ctx.enter_context(tc.tile_pool(name="raw", bufs=1))
         codes = ctx.enter_context(tc.tile_pool(name="codes", bufs=1))
-        stage = ctx.enter_context(tc.tile_pool(name="stage", bufs=2))
-        heads = ctx.enter_context(tc.tile_pool(name="heads", bufs=LOOKAHEAD + 2))
+        stage = ctx.enter_context(tc.tile_pool(name="stage", bufs=3))
         results = ctx.enter_context(tc.tile_pool(name="results", bufs=2))
-        psum = ctx.enter_context(tc.psum_pool(name="psum", bufs=4))
+        psum = ctx.enter_context(tc.psum_pool(name="psum", bufs=1))
 
         wdq_raw = raw.tile([P, PACK, C], BF16)
-        wdq_rows = W_dq.rearrange("(u p e) c -> u p (e c)", u=2, e=2)
-        for u in range(2):
-            nc.sync.dma_start(out=wdq_raw[:, 2 * u : 2 * u + 2, :].rearrange("p e c -> p (e c)"), in_=wdq_rows[u])
+        wdq_rows = W_dq.rearrange("(u p e) c -> u e p c", u=2, e=2)
+        for j in range(PACK):
+            nc.sync.dma_start(out=wdq_raw[:, j, :], in_=wdq_rows[j // 2, j % 2])
         x_raw = raw.tile([P, T_TILES, C], BF16)
         x_rows = x.flatten_outer_dims().rearrange("(p r) c -> r p c", r=T_TILES)
         for r in range(T_TILES):
             nc.sync.dma_start(out=x_raw[:, r, :], in_=x_rows[r])
         wuq_raw = raw.tile([P, PACK, NH * HS], BF16)
-        wuq_rows = W_uq.rearrange("(u p k) b -> u p (k b)", u=2, k=8)
-        for u in range(2):
-            nc.sync.dma_start(out=wuq_raw[:, 2 * u : 2 * u + 2, :].rearrange("p e c -> p (e c)"), in_=wuq_rows[u])
+        wuq_rows = W_uq.rearrange("(l a) b -> l (a b)", a=4).rearrange("(u p e) c -> u p e c", u=2, e=2)
         wuk_raw = raw.tile([P, NH, N], BF16)
         wuk_rows = W_uk.rearrange("(h d) n -> d h n", d=HS)
         wqr_raw = raw.tile([P, O // 256, 2 * L], BF16)
         wqr_rows = W_qr.rearrange("(a p e) l -> p a (e l)", p=P, e=2)
         cos_raw = const.tile([P, T_TILES, HS // 2], BF16)
         sin_raw = const.tile([P, T_TILES, HS // 2], BF16)
-        for b in range(O_BLOCKS):
+
+        def load_a(first_head, end_head):
+            a_cols = slice(HS * first_head, HS * end_head)
+            for u in range(2):
+                nc.sync.dma_start(out=wuq_raw[:, 2 * u : 2 * u + 2, a_cols], in_=wuq_rows[u][:, :, a_cols])
+
+        def load_block(b):
             nc.sync.dma_start(out=wuk_raw[:, 4 * b : 4 * b + 4, :], in_=wuk_rows[:, 4 * b : 4 * b + 4, :])
             nc.sync.dma_start(out=wqr_raw[:, 2 * b : 2 * b + 2, :], in_=wqr_rows[:, 2 * b : 2 * b + 2, :])
-            if b == 0:
-                nc.sync.dma_start(out=cos_raw[:], in_=cos.rearrange("(p r) i -> p r i", r=T_TILES))
-                nc.sync.dma_start(out=sin_raw[:], in_=sin.rearrange("(p r) i -> p r i", r=T_TILES))
+
+        load_a(0, FIRST_HEADS)
+        load_block(0)
+        nc.sync.dma_start(out=cos_raw[:], in_=cos.rearrange("(p r) i -> p r i", r=T_TILES))
+        nc.sync.dma_start(out=sin_raw[:], in_=sin.rearrange("(p r) i -> p r i", r=T_TILES))
+        load_a(FIRST_HEADS, NH)
+        for b in range(1, O_BLOCKS):
+            load_block(b)
 
         ident_f32 = const.tile([P, P], F32)
         make_identity(nc, ident_f32[:])
@@ -85,21 +97,12 @@ def tile_causalselfattention_pa_kernel(tc, x, cos, sin, W_dq, W_uq, W_uk, W_qr, 
                     scalar1=(-1.0 if e == 0 else 1.0), scalar2=0.0, op0=MULT, op1=ADD,
                 )
 
-        copies = [0]
-
-        def leave_psum(out, in_):
-            if copies[0] % VECTOR_EVERY == VECTOR_EVERY - 1:
-                nc.vector.tensor_copy(out=out, in_=in_)
-            else:
-                nc.scalar.copy(out=out, in_=in_)
-            copies[0] += 1
-
-        def transpose_words(grouped, rows_a, rows_b, tag):
-            bank = psum.tile([P, 2, 2, P], F32, tag=tag, name="words")
+        def transpose_words(grouped, rows_a, rows_b, banks):
+            bank = psum.tile([P, 2, 2, P], F32, tag=banks[0], bufs=banks[1], name="words")
             for run, rows in enumerate((rows_a, rows_b)):
                 for half in range(2):
                     nc.tensor.transpose(bank[:, run, half, :], rows.bitcast(F32)[:, P * half : P * half + P], ident_f32[:])
-            leave_psum(
+            nc.scalar.copy(
                 out=grouped.bitcast(F32).rearrange("p (a c) w -> p a c w", a=2),
                 in_=bank[:].rearrange("p a w c -> p a c w"),
             )
@@ -107,108 +110,117 @@ def tile_causalselfattention_pa_kernel(tc, x, cos, sin, W_dq, W_uq, W_uk, W_qr, 
         def quantise(grouped, words, scales):
             nc.vector.quantize_mx(out=words.bitcast(FP8X4), scales=scales, in_=grouped.rearrange("p c k -> p (c k)"))
 
-        wdq_words = codes.tile([P, 2, C_PASSES * 2 * P], U32, align_bytes=64)
-        wdq_scales = codes.tile([P, 2, C_PASSES * 2 * P], U8, align_bytes=64)
-        for u in range(2):
+        def quantise_rows(rows, words, scales):
+            grouped = stage.tile([P, C_PASSES * P, PACK], BF16, align_bytes=64)
             for pair in range(C_PASSES // 2):
-                wdq_grouped = stage.tile([P, 4 * P, PACK], BF16, align_bytes=64)
-                for g in (2 * pair, 2 * pair + 1):
-                    k_cols = slice(512 * g, 512 * g + 512)
-                    transpose_words(
-                        wdq_grouped[:, 256 * (g % 2) : 256 * (g % 2) + 256, :],
-                        wdq_raw[:, 2 * u, k_cols], wdq_raw[:, 2 * u + 1, k_cols], "a",
-                    )
-                cols = slice(512 * pair, 512 * pair + 512)
-                quantise(wdq_grouped[:], wdq_words[:, u, cols], wdq_scales[:, u, cols])
+                transpose_words(
+                    grouped[:, 256 * pair : 256 * pair + 256, :],
+                    rows[:, 1024 * pair : 1024 * pair + 512], rows[:, 1024 * pair + 512 : 1024 * pair + 1024], QA_BANKS,
+                )
+            quantise(grouped[:], words, scales)
 
+        wdq_words = codes.tile([P, PACK, C_PASSES * P], U32, align_bytes=64)
+        wdq_scales = codes.tile([P, PACK, C_PASSES * P], U8, align_bytes=64)
         x_words = codes.tile([P, T_TILES, C_PASSES * P], U32, align_bytes=64)
         x_scales = codes.tile([P, T_TILES, C_PASSES * P], U8, align_bytes=64)
         cq_words = codes.tile([P, T], U32, align_bytes=64)
         cq_scales = codes.tile([P, T], U8, align_bytes=64)
-        for r in range(T_TILES):
-            x_grouped = stage.tile([P, C_PASSES * P, PACK], BF16, align_bytes=64)
-            for pair in range(C_PASSES // 2):
-                transpose_words(
-                    x_grouped[:, 256 * pair : 256 * pair + 256, :],
-                    x_raw[:, r, 1024 * pair : 1024 * pair + 512], x_raw[:, r, 1024 * pair + 512 : 1024 * pair + 1024], "a",
-                )
-            quantise(x_grouped[:], x_words[:, r, :], x_scales[:, r, :])
-            cq_bank = psum.tile([P, PACK, P], F32, tag="b")
+
+        def make_c_q(r):
+            cq_bank = psum.tile([P, PACK, P], F32, tag=KE_BANKS[0], bufs=KE_BANKS[1])
             for j in range(PACK):
                 for g in range(C_PASSES):
-                    l_cols = slice(256 * g + P * (j % 2), 256 * g + P * (j % 2) + P)
-                    t_cols = slice(P * g, P * g + P)
+                    k_cols = slice(P * g, P * g + P)
                     nc.tensor.matmul_mx(
                         out=cq_bank[:, j, :],
-                        lhsT=wdq_words[:, j // 2, l_cols].bitcast(FP8X4), lhsT_scale=wdq_scales[:, j // 2, l_cols],
-                        rhs=x_words[:, r, t_cols].bitcast(FP8X4), rhs_scale=x_scales[:, r, t_cols],
+                        lhsT=wdq_words[:, j, k_cols].bitcast(FP8X4), lhsT_scale=wdq_scales[:, j, k_cols],
+                        rhs=x_words[:, r, k_cols].bitcast(FP8X4), rhs_scale=x_scales[:, r, k_cols],
                         start=(g == 0), stop=(g == C_PASSES - 1),
                     )
             cq_grouped = stage.tile([P, P, PACK], BF16, align_bytes=64)
-            leave_psum(out=cq_grouped[:], in_=cq_bank[:].rearrange("p j t -> p t j"))
+            nc.vector.tensor_copy(out=cq_grouped[:], in_=cq_bank[:].rearrange("p j t -> p t j"))
             quantise(cq_grouped[:], cq_words[:, P * r : P * r + P], cq_scales[:, P * r : P * r + P])
 
         wqr_words = codes.tile([P, O], U32, align_bytes=64)
         wqr_scales = codes.tile([P, O], U8, align_bytes=64)
+        wqr_grouped = {}
+
+        def transpose_wqr(b, a, banks):
+            if a == 0:
+                wqr_grouped[b] = stage.tile([P, BANK, PACK], BF16, align_bytes=64, name="wqr_grouped", bufs=2)
+            transpose_words(
+                wqr_grouped[b][:, 256 * a : 256 * a + 256, :],
+                wqr_raw[:, 2 * b + a, 0:L], wqr_raw[:, 2 * b + a, L : 2 * L], banks,
+            )
 
         def quantise_wqr(b):
-            wqr_grouped = stage.tile([P, 512, PACK], BF16, align_bytes=64)
-            for a in range(2):
-                transpose_words(
-                    wqr_grouped[:, 256 * a : 256 * a + 256, :],
-                    wqr_raw[:, 2 * b + a, 0:L], wqr_raw[:, 2 * b + a, L : 2 * L], "b",
-                )
-            cols = slice(512 * b, 512 * b + 512)
-            quantise(wqr_grouped[:], wqr_words[:, cols], wqr_scales[:, cols])
+            cols = slice(BANK * b, BANK * b + BANK)
+            quantise(wqr_grouped[b][:], wqr_words[:, cols], wqr_scales[:, cols])
 
+        a_t = {}
+
+        def transpose_a(h, banks):
+            at_bank = psum.tile([P, PACK, P], BF16, tag=banks[0], bufs=banks[1])
+            for j in range(PACK):
+                nc.tensor.transpose(at_bank[:, j, :], wuq_raw[:, j, HS * h : HS * h + HS], ident_bf16[:])
+            a_t[h] = stage.tile([P, PACK, P], BF16, name="a_t", bufs=5)
+            nc.scalar.copy(out=a_t[h][:], in_=at_bank[:])
+
+        ke_grouped = {}
         ke_words = {}
         ke_scales = {}
 
-        def make_k_eff(h):
-            at_bank = psum.tile([P, PACK, P], BF16, tag="b")
+        def make_k_eff(h, i):
+            if i == 0:
+                ke_grouped[h] = stage.tile([P, N, PACK], BF16, align_bytes=64, name="ke_grouped")
+            ke_bank = psum.tile([P, PACK, P], F32, tag=KE_BANKS[0], bufs=KE_BANKS[1])
             for j in range(PACK):
-                nc.tensor.transpose(at_bank[:, j, :], wuq_raw[:, j, HS * h : HS * h + HS], ident_bf16[:])
-            a_t = stage.tile([P, PACK, P], BF16)
-            leave_psum(out=a_t[:], in_=at_bank[:])
-            ke_grouped = stage.tile([P, N, PACK], BF16, align_bytes=64)
-            for n0 in range(0, N, P):
-                ke_bank = psum.tile([P, PACK, P], F32, tag="b")
-                for j in range(PACK):
-                    nc.tensor.matmul(ke_bank[:, j, :], lhsT=a_t[:, j, :], rhs=wuk_raw[:, h, n0 : n0 + P], start=True, stop=True)
-                leave_psum(out=ke_grouped[:, n0 : n0 + P, :], in_=ke_bank[:].rearrange("p j n -> p n j"))
-            ke_words[h] = heads.tile([P, N], U32, align_bytes=64, name="ke_words")
-            ke_scales[h] = heads.tile([P, N], U8, align_bytes=64, name="ke_scales")
-            quantise(ke_grouped[:], ke_words[h][:], ke_scales[h][:])
+                nc.tensor.matmul(ke_bank[:, j, :], lhsT=a_t[h][:, j, :], rhs=wuk_raw[:, h, P * i : P * i + P], start=True, stop=True)
+            if i == 3:
+                nc.scalar.copy(out=ke_grouped[h][:, P * i : P * i + P, :], in_=ke_bank[:].rearrange("p j n -> p n j"))
+            else:
+                nc.vector.tensor_copy(out=ke_grouped[h][:, P * i : P * i + P, :], in_=ke_bank[:].rearrange("p j n -> p n j"))
+
+        def quantise_k_eff(h):
+            ke_words[h] = stage.tile([P, N], U32, align_bytes=64, name="ke_words")
+            ke_scales[h] = stage.tile([P, N], U8, align_bytes=64, name="ke_scales")
+            quantise(ke_grouped[h][:], ke_words[h][:], ke_scales[h][:])
 
         q_abs_rows = out_0.flatten_outer_dims().rearrange("(h p r) n -> h p r n", h=NH, r=T_TILES)
+        q_abs = {}
 
-        def make_q_abs(h):
-            q_abs = results.tile([P, T_TILES, N], F32, bufs=3)
-            for r in range(T_TILES):
-                qa_bank = psum.tile([P, N], F32, tag="a")
-                nc.tensor.matmul_mx(
-                    out=qa_bank[:],
-                    lhsT=cq_words[:, P * r : P * r + P].bitcast(FP8X4), lhsT_scale=cq_scales[:, P * r : P * r + P],
-                    rhs=ke_words[h][:].bitcast(FP8X4), rhs_scale=ke_scales[h][:],
-                    start=True, stop=True,
-                )
-                leave_psum(out=q_abs[:, r, :], in_=qa_bank[:])
-            nc.sync.dma_start(out=q_abs_rows[h], in_=q_abs[:])
+        def make_q_abs(h, r):
+            if r == 0:
+                q_abs[h] = results.tile([P, T_TILES, N], F32, name="q_abs", bufs=3)
+            qa_bank = psum.tile([P, N], F32, tag=QA_BANKS[0], bufs=QA_BANKS[1])
+            nc.tensor.matmul_mx(
+                out=qa_bank[:],
+                lhsT=cq_words[:, P * r : P * r + P].bitcast(FP8X4), lhsT_scale=cq_scales[:, P * r : P * r + P],
+                rhs=ke_words[h][:].bitcast(FP8X4), rhs_scale=ke_scales[h][:],
+                start=True, stop=True,
+            )
+            nc.scalar.copy(out=q_abs[h][:, r, :], in_=qa_bank[:])
+            if r == T_TILES - 1:
+                nc.sync.dma_start(out=q_abs_rows[h], in_=q_abs[h][:])
 
         q_r_rows = out_1.rearrange("b t h d -> (b t) (h d)").rearrange("(p r) o -> p r o", r=T_TILES)
-        q_r = {}
+        c_qr = {}
 
-        def make_q_r(b, r):
-            if r == 0:
-                q_r[b] = results.tile([P, T_TILES, 512], F32, name="q_r")
-            cols = slice(512 * b, 512 * b + 512)
-            cr_bank = psum.tile([P, 2, 2, P], F32, tag="a")
+        def make_c_qr(bank_no):
+            b, r = divmod(bank_no, T_TILES)
+            cols = slice(BANK * b, BANK * b + BANK)
+            c_qr[bank_no] = psum.tile([P, 2, 2, P], F32, tag="cr", bufs=1, name="cr_bank")
             nc.tensor.matmul_mx(
-                out=cr_bank[:].rearrange("p a e c -> p (a e c)"),
+                out=c_qr[bank_no][:].rearrange("p a e c -> p (a e c)"),
                 lhsT=cq_words[:, P * r : P * r + P].bitcast(FP8X4), lhsT_scale=cq_scales[:, P * r : P * r + P],
                 rhs=wqr_words[:, cols].bitcast(FP8X4), rhs_scale=wqr_scales[:, cols],
                 start=True, stop=True,
             )
+
+        def rotate(bank_no):
+            b, r = divmod(bank_no, T_TILES)
+            cr_bank = c_qr[bank_no]
+            q_r = results.tile([P, BANK], F32, bufs=3)
             same = results.tile([P, 2, P, 2], F32)
             nc.vector.tensor_tensor(
                 out=same[:], in0=cr_bank[:].rearrange("p a e c -> p a c e"),
@@ -221,19 +233,45 @@ def tile_causalselfattention_pa_kernel(tc, x, cos, sin, W_dq, W_uq, W_uk, W_qr, 
                     in1=sin_signed[:, r, e, :].unsqueeze(1).to_broadcast([P, 2, P]), op=MULT,
                 )
             nc.gpsimd.tensor_tensor(
-                out=q_r[b][:, r, :].rearrange("p (a c e) -> p a c e", a=2, e=2),
+                out=q_r[:].rearrange("p (a c e) -> p a c e", a=2, e=2),
                 in0=same[:], in1=cross[:].rearrange("p e a c -> p a c e"), op=ADD,
             )
-            if r == T_TILES - 1:
-                nc.sync.dma_start(out=q_r_rows[:, :, cols], in_=q_r[b][:])
+            nc.sync.dma_start(out=q_r_rows[:, r, BANK * b : BANK * b + BANK], in_=q_r[:])
 
-        for h in range(LOOKAHEAD):
-            make_k_eff(h)
+        for j in range(PACK):
+            quantise_rows(wdq_raw[:, j, :], wdq_words[:, j, :], wdq_scales[:, j, :])
+        for r in range(T_TILES + 1):
+            if r < T_TILES:
+                quantise_rows(x_raw[:, r, :], x_words[:, r, :], x_scales[:, r, :])
+            else:
+                for h in range(4):
+                    transpose_a(h, QA_BANKS)
+            if r > 0:
+                make_c_q(r - 1)
+        for a in range(2):
+            transpose_wqr(0, a, QA_BANKS)
+        for i in range(4):
+            make_k_eff(0, i)
         quantise_wqr(0)
+        quantise_k_eff(0)
+        for i in range(4):
+            make_k_eff(1, i)
+        make_c_qr(0)
+
         for h in range(NH):
-            if h + LOOKAHEAD < NH:
-                make_k_eff(h + LOOKAHEAD)
-            make_q_abs(h)
-            make_q_r(h // T_TILES, h % T_TILES)
-            if h % T_TILES == 1 and h // T_TILES + 1 < O_BLOCKS:
-                quantise_wqr(h // T_TILES + 1)
+            next_block = h // T_TILES + 1
+            if h + 4 < NH:
+                transpose_a(h + 4, TP_BANKS)
+            rotate(h)
+            if h + 1 < NH:
+                quantise_k_eff(h + 1)
+            if h % T_TILES == 2 and next_block < O_BLOCKS:
+                quantise_wqr(next_block)
+            for i in range(4):
+                make_q_abs(h, i)
+                if i == 3 and h + 1 < NH:
+                    make_c_qr(h + 1)
+                if h + 2 < NH:
+                    make_k_eff(h + 2, i)
+                if i == 1 and h % T_TILES < 2 and next_block < O_BLOCKS:
+                    transpose_wqr(next_block, h % T_TILES, TP_BANKS)

@@ -97,6 +97,12 @@ def tile_causalselfattention_pa_kernel(tc, x, cos, sin, W_dq, W_uq, W_uk, W_qr, 
                     scalar1=(-1.0 if e == 0 else 1.0), scalar2=0.0, op0=MULT, op1=ADD,
                 )
 
+        def leave_psum(on_scalar, out, in_):
+            if on_scalar:
+                nc.scalar.copy(out=out, in_=in_)
+            else:
+                nc.vector.tensor_copy(out=out, in_=in_)
+
         def transpose_words(grouped, rows_a, rows_b, banks):
             bank = psum.tile([P, 2, 2, P], F32, tag=banks[0], bufs=banks[1], name="words")
             for run, rows in enumerate((rows_a, rows_b)):
@@ -138,7 +144,7 @@ def tile_causalselfattention_pa_kernel(tc, x, cos, sin, W_dq, W_uq, W_uk, W_qr, 
                         start=(g == 0), stop=(g == C_PASSES - 1),
                     )
             cq_grouped = stage.tile([P, P, PACK], BF16, align_bytes=64)
-            nc.vector.tensor_copy(out=cq_grouped[:], in_=cq_bank[:].rearrange("p j t -> p t j"))
+            leave_psum(r % 2 == 1, out=cq_grouped[:], in_=cq_bank[:].rearrange("p j t -> p t j"))
             quantise(cq_grouped[:], cq_words[:, P * r : P * r + P], cq_scales[:, P * r : P * r + P])
 
         wqr_words = codes.tile([P, O], U32, align_bytes=64)
@@ -170,16 +176,13 @@ def tile_causalselfattention_pa_kernel(tc, x, cos, sin, W_dq, W_uq, W_uk, W_qr, 
         ke_words = {}
         ke_scales = {}
 
-        def make_k_eff(h, i):
+        def make_k_eff(h, i, on_scalar):
             if i == 0:
                 ke_grouped[h] = stage.tile([P, N, PACK], BF16, align_bytes=64, name="ke_grouped")
             ke_bank = psum.tile([P, PACK, P], F32, tag=KE_BANKS[0], bufs=KE_BANKS[1])
             for j in range(PACK):
                 nc.tensor.matmul(ke_bank[:, j, :], lhsT=a_t[h][:, j, :], rhs=wuk_raw[:, h, P * i : P * i + P], start=True, stop=True)
-            if i == 3:
-                nc.scalar.copy(out=ke_grouped[h][:, P * i : P * i + P, :], in_=ke_bank[:].rearrange("p j n -> p n j"))
-            else:
-                nc.vector.tensor_copy(out=ke_grouped[h][:, P * i : P * i + P, :], in_=ke_bank[:].rearrange("p j n -> p n j"))
+            leave_psum(on_scalar, out=ke_grouped[h][:, P * i : P * i + P, :], in_=ke_bank[:].rearrange("p j n -> p n j"))
 
         def quantise_k_eff(h):
             ke_words[h] = stage.tile([P, N], U32, align_bytes=64, name="ke_words")
@@ -240,22 +243,23 @@ def tile_causalselfattention_pa_kernel(tc, x, cos, sin, W_dq, W_uq, W_uk, W_qr, 
 
         for j in range(PACK):
             quantise_rows(wdq_raw[:, j, :], wdq_words[:, j, :], wdq_scales[:, j, :])
-        for r in range(T_TILES + 1):
+        for r in range(T_TILES + 2):
             if r < T_TILES:
                 quantise_rows(x_raw[:, r, :], x_words[:, r, :], x_scales[:, r, :])
-            else:
-                for h in range(4):
-                    transpose_a(h, QA_BANKS)
-            if r > 0:
-                make_c_q(r - 1)
-        for a in range(2):
-            transpose_wqr(0, a, QA_BANKS)
+            if r == T_TILES - 1:
+                transpose_a(0, QA_BANKS)
+            if r >= 2:
+                make_c_q(r - 2)
         for i in range(4):
-            make_k_eff(0, i)
+            make_k_eff(0, i, False)
+            if i % 2 == 1:
+                transpose_wqr(0, i // 2, QA_BANKS)
+        for h in range(1, 4):
+            transpose_a(h, QA_BANKS)
         quantise_wqr(0)
         quantise_k_eff(0)
         for i in range(4):
-            make_k_eff(1, i)
+            make_k_eff(1, i, True)
         make_c_qr(0)
 
         for h in range(NH):
@@ -272,6 +276,6 @@ def tile_causalselfattention_pa_kernel(tc, x, cos, sin, W_dq, W_uq, W_uk, W_qr, 
                 if i == 3 and h + 1 < NH:
                     make_c_qr(h + 1)
                 if h + 2 < NH:
-                    make_k_eff(h + 2, i)
+                    make_k_eff(h + 2, i, i == 3 or (i == 0 and h % T_TILES == 2))
                 if i == 1 and h % T_TILES < 2 and next_block < O_BLOCKS:
                     transpose_wqr(next_block, h % T_TILES, TP_BANKS)

@@ -252,10 +252,11 @@ def tile_causalselfattention_pa_kernel(tc, x, cos, sin, W_dq, W_uq, W_uk, W_qr, 
                 make_c_q(r - 2)
         for i in range(4):
             make_k_eff(0, i, False)
-            if i % 2 == 1:
-                transpose_wqr(0, i // 2, QA_BANKS)
-        for h in range(1, 4):
-            transpose_a(h, QA_BANKS)
+            if i < 2:
+                transpose_wqr(0, i, QA_BANKS)
+            else:
+                transpose_a(i - 1, QA_BANKS)
+        transpose_a(3, QA_BANKS)
         quantise_wqr(0)
         quantise_k_eff(0)
         for i in range(4):

@@ -35,7 +35,6 @@ FLOPS = 2 * (T * C * L + NH * L * HS * N + NH * T * L * N + T * L * O)
 def tile_causalselfattention_pa_kernel(tc, x, cos, sin, W_dq, W_uq, W_uk, W_qr, out_0, out_1):
     nc = tc.nc
     with ExitStack() as ctx:
-        ctx.enter_context(tc.manual_schedule())
         const = ctx.enter_context(tc.tile_pool(name="const", bufs=1))
         raw = ctx.enter_context(tc.tile_pool(name="raw", bufs=1))
         codes = ctx.enter_context(tc.tile_pool(name="codes", bufs=1))

from contextlib import ExitStack

import concourse.mybir as mybir
from concourse.masks import make_identity

F32 = mybir.dt.float32
BF16 = mybir.dt.bfloat16
U32 = mybir.dt.uint32
U8 = mybir.dt.uint8
FP8X4 = mybir.dt.float8_e4m3fn_x4
MULT = mybir.AluOpType.mult
ADD = mybir.AluOpType.add

P = 128
PACK = 4
T = 512
C = 2048
L = 512
NH = 16
HS = 128
N = 512
O = 2048
C_PASSES = C // (P * PACK)
T_TILES = T // P
BANK = 512
O_BLOCKS = O // BANK
FIRST_HEADS = 4
QA_BANKS = ("qa", 3)
KE_BANKS = ("ke", 3)
TP_BANKS = ("tp", 1)

FLOPS = 2 * (T * C * L + NH * L * HS * N + NH * T * L * N + T * L * O)


def tile_causalselfattention_pa_kernel(tc, x, cos, sin, W_dq, W_uq, W_uk, W_qr, out_0, out_1):
    nc = tc.nc
    with ExitStack() as ctx:
        const = ctx.enter_context(tc.tile_pool(name="const", bufs=1))
        raw = ctx.enter_context(tc.tile_pool(name="raw", bufs=1))
        codes = ctx.enter_context(tc.tile_pool(name="codes", bufs=1))
        stage = ctx.enter_context(tc.tile_pool(name="stage", bufs=3))
        results = ctx.enter_context(tc.tile_pool(name="results", bufs=2))
        psum = ctx.enter_context(tc.psum_pool(name="psum", bufs=1))

        wdq_raw = raw.tile([P, PACK, C], BF16)
        wdq_rows = W_dq.rearrange("(u p e) c -> u e p c", u=2, e=2)
        for j in range(PACK):
            nc.sync.dma_start(out=wdq_raw[:, j, :], in_=wdq_rows[j // 2, j % 2])
        x_raw = raw.tile([P, T_TILES, C], BF16)
        x_rows = x.flatten_outer_dims().rearrange("(p r) c -> r p c", r=T_TILES)
        for r in range(T_TILES):
            nc.sync.dma_start(out=x_raw[:, r, :], in_=x_rows[r])
        wuq_raw = raw.tile([P, PACK, NH * HS], BF16)
        wuq_rows = W_uq.rearrange("(l a) b -> l (a b)", a=4).rearrange("(u p e) c -> u p e c", u=2, e=2)
        wuk_raw = raw.tile([P, NH, N], BF16)
        wuk_rows = W_uk.rearrange("(h d) n -> d h n", d=HS)
        wqr_raw = raw.tile([P, O // 256, 2 * L], BF16)
        wqr_rows = W_qr.rearrange("(a p e) l -> p a (e l)", p=P, e=2)
        cos_raw = const.tile([P, T_TILES, HS // 2], BF16)
        sin_raw = const.tile([P, T_TILES, HS // 2], BF16)

        def load_a(first_head, end_head):
            a_cols = slice(HS * first_head, HS * end_head)
            for u in range(2):
                nc.sync.dma_start(out=wuq_raw[:, 2 * u : 2 * u + 2, a_cols], in_=wuq_rows[u][:, :, a_cols])

        def load_block(b):
            nc.sync.dma_start(out=wuk_raw[:, 4 * b : 4 * b + 4, :], in_=wuk_rows[:, 4 * b : 4 * b + 4, :])
            nc.sync.dma_start(out=wqr_raw[:, 2 * b : 2 * b + 2, :], in_=wqr_rows[:, 2 * b : 2 * b + 2, :])

        load_a(0, FIRST_HEADS)
        load_block(0)
        nc.sync.dma_start(out=cos_raw[:], in_=cos.rearrange("(p r) i -> p r i", r=T_TILES))
        nc.sync.dma_start(out=sin_raw[:], in_=sin.rearrange("(p r) i -> p r i", r=T_TILES))
        load_a(FIRST_HEADS, NH)
        for b in range(1, O_BLOCKS):
            load_block(b)

        ident_f32 = const.tile([P, P], F32)
        make_identity(nc, ident_f32[:])
        ident_bf16 = const.tile([P, P], BF16)
        make_identity(nc, ident_bf16[:])

        cos_pairs = const.tile([P, T_TILES, P, 2], F32)
        sin_signed = const.tile([P, T_TILES, 2, P], F32)
        for r in range(T_TILES):
            nc.gpsimd.tensor_scalar(
                out=cos_pairs[:, r].rearrange("p (a i) e -> p a i e", a=2),
                in0=cos_raw[:, r, :].unsqueeze(1).unsqueeze(3).to_broadcast([P, 2, HS // 2, 2]),
                scalar1=1.0, scalar2=0.0, op0=MULT, op1=ADD,
            )
            for e in range(2):
                nc.gpsimd.tensor_scalar(
                    out=sin_signed[:, r, e, :].rearrange("p (a i) -> p a i", a=2),
                    in0=sin_raw[:, r, :].unsqueeze(1).to_broadcast([P, 2, HS // 2]),
                    scalar1=(-1.0 if e == 0 else 1.0), scalar2=0.0, op0=MULT, op1=ADD,
                )

        def leave_psum(on_scalar, out, in_):
            if on_scalar:
                nc.scalar.copy(out=out, in_=in_)
            else:
                nc.vector.tensor_copy(out=out, in_=in_)

        def transpose_words(grouped, rows_a, rows_b, banks):
            bank = psum.tile([P, 2, 2, P], F32, tag=banks[0], bufs=banks[1], name="words")
            for run, rows in enumerate((rows_a, rows_b)):
                for half in range(2):
                    nc.tensor.transpose(bank[:, run, half, :], rows.bitcast(F32)[:, P * half : P * half + P], ident_f32[:])
            nc.scalar.copy(
                out=grouped.bitcast(F32).rearrange("p (a c) w -> p a c w", a=2),
                in_=bank[:].rearrange("p a w c -> p a c w"),
            )

        def quantise(grouped, words, scales):
            nc.vector.quantize_mx(out=words.bitcast(FP8X4), scales=scales, in_=grouped.rearrange("p c k -> p (c k)"))

        def quantise_rows(rows, words, scales):
            grouped = stage.tile([P, C_PASSES * P, PACK], BF16, align_bytes=64)
            for pair in range(C_PASSES // 2):
                transpose_words(
                    grouped[:, 256 * pair : 256 * pair + 256, :],
                    rows[:, 1024 * pair : 1024 * pair + 512], rows[:, 1024 * pair + 512 : 1024 * pair + 1024], QA_BANKS,
                )
            quantise(grouped[:], words, scales)

        wdq_words = codes.tile([P, PACK, C_PASSES * P], U32, align_bytes=64)
        wdq_scales = codes.tile([P, PACK, C_PASSES * P], U8, align_bytes=64)
        x_words = codes.tile([P, T_TILES, C_PASSES * P], U32, align_bytes=64)
        x_scales = codes.tile([P, T_TILES, C_PASSES * P], U8, align_bytes=64)
        cq_words = codes.tile([P, T], U32, align_bytes=64)
        cq_scales = codes.tile([P, T], U8, align_bytes=64)

        def make_c_q(r):
            cq_bank = psum.tile([P, PACK, P], F32, tag=KE_BANKS[0], bufs=KE_BANKS[1])
            for j in range(PACK):
                for g in range(C_PASSES):
                    k_cols = slice(P * g, P * g + P)
                    nc.tensor.matmul_mx(
                        out=cq_bank[:, j, :],
                        lhsT=wdq_words[:, j, k_cols].bitcast(FP8X4), lhsT_scale=wdq_scales[:, j, k_cols],
                        rhs=x_words[:, r, k_cols].bitcast(FP8X4), rhs_scale=x_scales[:, r, k_cols],
                        start=(g == 0), stop=(g == C_PASSES - 1),
                    )
            cq_grouped = stage.tile([P, P, PACK], BF16, align_bytes=64)
            leave_psum(r % 2 == 1, out=cq_grouped[:], in_=cq_bank[:].rearrange("p j t -> p t j"))
            quantise(cq_grouped[:], cq_words[:, P * r : P * r + P], cq_scales[:, P * r : P * r + P])

        wqr_words = codes.tile([P, O], U32, align_bytes=64)
        wqr_scales = codes.tile([P, O], U8, align_bytes=64)
        wqr_grouped = {}

        def transpose_wqr(b, a, banks):
            if a == 0:
                wqr_grouped[b] = stage.tile([P, BANK, PACK], BF16, align_bytes=64, name="wqr_grouped", bufs=2)
            transpose_words(
                wqr_grouped[b][:, 256 * a : 256 * a + 256, :],
                wqr_raw[:, 2 * b + a, 0:L], wqr_raw[:, 2 * b + a, L : 2 * L], banks,
            )

        def quantise_wqr(b):
            cols = slice(BANK * b, BANK * b + BANK)
            quantise(wqr_grouped[b][:], wqr_words[:, cols], wqr_scales[:, cols])

        a_t = {}

        def transpose_a(h, banks):
            at_bank = psum.tile([P, PACK, P], BF16, tag=banks[0], bufs=banks[1])
            for j in range(PACK):
                nc.tensor.transpose(at_bank[:, j, :], wuq_raw[:, j, HS * h : HS * h + HS], ident_bf16[:])
            a_t[h] = stage.tile([P, PACK, P], BF16, name="a_t", bufs=5)
            nc.scalar.copy(out=a_t[h][:], in_=at_bank[:])

        ke_grouped = {}
        ke_words = {}
        ke_scales = {}

        def make_k_eff(h, i, on_scalar):
            if i == 0:
                ke_grouped[h] = stage.tile([P, N, PACK], BF16, align_bytes=64, name="ke_grouped")
            ke_bank = psum.tile([P, PACK, P], F32, tag=KE_BANKS[0], bufs=KE_BANKS[1])
            for j in range(PACK):
                nc.tensor.matmul(ke_bank[:, j, :], lhsT=a_t[h][:, j, :], rhs=wuk_raw[:, h, P * i : P * i + P], start=True, stop=True)
            leave_psum(on_scalar, out=ke_grouped[h][:, P * i : P * i + P, :], in_=ke_bank[:].rearrange("p j n -> p n j"))

        def quantise_k_eff(h):
            ke_words[h] = stage.tile([P, N], U32, align_bytes=64, name="ke_words")
            ke_scales[h] = stage.tile([P, N], U8, align_bytes=64, name="ke_scales")
            quantise(ke_grouped[h][:], ke_words[h][:], ke_scales[h][:])

        q_abs_rows = out_0.flatten_outer_dims().rearrange("(h p r) n -> h p r n", h=NH, r=T_TILES)
        q_abs = {}

        def make_q_abs(h, r):
            if r == 0:
                q_abs[h] = results.tile([P, T_TILES, N], F32, name="q_abs", bufs=3)
            qa_bank = psum.tile([P, N], F32, tag=QA_BANKS[0], bufs=QA_BANKS[1])
            nc.tensor.matmul_mx(
                out=qa_bank[:],
                lhsT=cq_words[:, P * r : P * r + P].bitcast(FP8X4), lhsT_scale=cq_scales[:, P * r : P * r + P],
                rhs=ke_words[h][:].bitcast(FP8X4), rhs_scale=ke_scales[h][:],
                start=True, stop=True,
            )
            nc.scalar.copy(out=q_abs[h][:, r, :], in_=qa_bank[:])
            if r == T_TILES - 1:
                nc.sync.dma_start(out=q_abs_rows[h], in_=q_abs[h][:])

        q_r_rows = out_1.rearrange("b t h d -> (b t) (h d)").rearrange("(p r) o -> p r o", r=T_TILES)
        c_qr = {}

        def make_c_qr(bank_no):
            b, r = divmod(bank_no, T_TILES)
            cols = slice(BANK * b, BANK * b + BANK)
            c_qr[bank_no] = psum.tile([P, 2, 2, P], F32, tag="cr", bufs=1, name="cr_bank")
            nc.tensor.matmul_mx(
                out=c_qr[bank_no][:].rearrange("p a e c -> p (a e c)"),
                lhsT=cq_words[:, P * r : P * r + P].bitcast(FP8X4), lhsT_scale=cq_scales[:, P * r : P * r + P],
                rhs=wqr_words[:, cols].bitcast(FP8X4), rhs_scale=wqr_scales[:, cols],
                start=True, stop=True,
            )

        def rotate(bank_no):
            b, r = divmod(bank_no, T_TILES)
            cr_bank = c_qr[bank_no]
            q_r = results.tile([P, BANK], F32, bufs=3)
            same = results.tile([P, 2, P, 2], F32)
            nc.vector.tensor_tensor(
                out=same[:], in0=cr_bank[:].rearrange("p a e c -> p a c e"),
                in1=cos_pairs[:, r].unsqueeze(1).to_broadcast([P, 2, P, 2]), op=MULT,
            )
            cross = results.tile([P, 2, 2, P], F32)
            for e in range(2):
                nc.vector.tensor_tensor(
                    out=cross[:, e], in0=cr_bank[:, :, 1 - e, :],
                    in1=sin_signed[:, r, e, :].unsqueeze(1).to_broadcast([P, 2, P]), op=MULT,
                )
            nc.gpsimd.tensor_tensor(
                out=q_r[:].rearrange("p (a c e) -> p a c e", a=2, e=2),
                in0=same[:], in1=cross[:].rearrange("p e a c -> p a c e"), op=ADD,
            )
            nc.sync.dma_start(out=q_r_rows[:, r, BANK * b : BANK * b + BANK], in_=q_r[:])

        for j in range(PACK):
            quantise_rows(wdq_raw[:, j, :], wdq_words[:, j, :], wdq_scales[:, j, :])
        for r in range(T_TILES + 2):
            if r < T_TILES:
                quantise_rows(x_raw[:, r, :], x_words[:, r, :], x_scales[:, r, :])
            if r == T_TILES - 1:
                transpose_a(0, QA_BANKS)
            if r >= 2:
                make_c_q(r - 2)
        for i in range(4):
            make_k_eff(0, i, False)
            if i < 2:
                transpose_wqr(0, i, QA_BANKS)
            else:
                transpose_a(i - 1, QA_BANKS)
        transpose_a(3, QA_BANKS)
        quantise_wqr(0)
        quantise_k_eff(0)
        for i in range(4):
            make_k_eff(1, i, True)
        make_c_qr(0)

        for h in range(NH):
            next_block = h // T_TILES + 1
            if h + 4 < NH:
                transpose_a(h + 4, TP_BANKS)
            rotate(h)
            if h + 1 < NH:
                quantise_k_eff(h + 1)
            if h % T_TILES == 2 and next_block < O_BLOCKS:
                quantise_wqr(next_block)
            for i in range(4):
                make_q_abs(h, i)
                if i == 3 and h + 1 < NH:
                    make_c_qr(h + 1)
                if h + 2 < NH:
                    make_k_eff(h + 2, i, i == 3 or (i == 0 and h % T_TILES == 2))
                if i == 1 and h % T_TILES < 2 and next_block < O_BLOCKS:
                    transpose_wqr(next_block, h % T_TILES, TP_BANKS)
